import numpy as np
import ml_dtypes


def mxq(x, axis, fmt="e4m3"):
    dtype, down = {"e4m3": (ml_dtypes.float8_e4m3fn, 7), "e5m2": (ml_dtypes.float8_e5m2, 14)}[fmt]
    v = np.moveaxis(np.asarray(x, np.float32).astype(ml_dtypes.bfloat16).astype(np.float64), axis, -1)
    blocks = v.reshape(v.shape[:-1] + (-1, 32))
    amax = np.abs(blocks).max(-1, keepdims=True)
    byte = np.maximum(np.where(amax > 0, np.frexp(amax)[1] - 1 + 127, 0) - down, 1)
    scale = np.exp2(byte - 127.0)
    codes = (blocks / scale).astype(np.float32).astype(dtype).astype(np.float64)
    return np.moveaxis((codes * scale).reshape(v.shape), -1, axis)


WIDE = False


def mx_kscale(k):
    if not WIDE:
        return np.ones(k)
    levels = np.array([10, -10, 5, -5, 0])
    a = np.random.permutation(np.resize(levels, k // 512 * 4)).reshape(k // 512, 4)
    idx = np.arange(k)
    return np.exp2(a[idx // 512, idx % 128 // 32])


BF16 = ml_dtypes.bfloat16


def bf(x):
    return np.asarray(x, np.float32).astype(BF16)


def f64(x):
    return np.asarray(x).astype(np.float64)


E2M1 = np.array([0.0, 0.5, 1.0, 1.5, 2.0, 3.0, 4.0, 6.0, -0.0, -0.5, -1.0, -1.5, -2.0, -3.0, -4.0, -6.0])


def pack_weight(w, fmt):
    k, n = w.shape
    w = f64(bf(w)).reshape(k // 32, 32, n)
    amax = np.abs(w).max(1)
    if fmt == "e4m3":
        byte = np.frexp(amax)[1] - 1 + 127 - 7
    else:
        mant, ex = np.frexp(amax / 6.0)
        byte = np.where(mant > 0.5, ex, ex - 1) + 127
    byte = np.clip(np.where(amax > 0, byte, 1), 1, 254)
    scaled = (w * np.exp2(127.0 - byte)[:, None, :]).reshape(k, n).astype(np.float32)
    by_word = np.ascontiguousarray(scaled.reshape(k // 512, 128, 4, n).transpose(0, 1, 3, 2))
    if fmt == "e4m3":
        words = by_word.astype(ml_dtypes.float8_e4m3fn).view(np.uint8)
    else:
        c = by_word.astype(ml_dtypes.float4_e2m1fn).view(np.uint8) & 0xF
        words = c[..., 0::2] | (c[..., 1::2] << 4)
    return np.ascontiguousarray(words), np.ascontiguousarray(byte.astype(np.uint8).reshape(k // 512, 16, n))


def unpack_weight(words, scales, fmt):
    g, p, n, _ = words.shape
    if fmt == "e4m3":
        vals = np.ascontiguousarray(words).view(ml_dtypes.float8_e4m3fn).astype(np.float64)
    else:
        nib = np.empty((g, p, n, 4), np.uint8)
        nib[..., 0::2] = words & 0xF
        nib[..., 1::2] = words >> 4
        vals = E2M1[nib]
    vals = vals * np.repeat(np.exp2(scales.astype(np.float64) - 127.0), 8, axis=1)[..., None]
    return vals.transpose(0, 1, 3, 2).reshape(g * 512, n)


B, S, H = 4, 1024, 512
GAMMA = 0.96875


def sigmoid(v):
    return 1.0 / (1.0 + np.exp(-v))


def setup_inputs():
    s, u = mx_kscale(H), mx_kscale(H)
    a = 1.4 / H ** 0.25
    q = bf(np.random.standard_normal((B, S, H)) * a * s)
    k = bf(np.random.standard_normal((B, S, H)) * a / s)
    x = bf(np.random.standard_normal((B, S, H)) * u)
    words, scales = pack_weight(np.random.standard_normal((H, H)) * 0.5 / np.sqrt(H) / u[:, None], "e4m3")
    return {"q": q, "k": k, "x": x, "w_v_words": words, "w_v_scales": scales}


def reference(q, k, x, w_v_words, w_v_scales):
    idx = f64(np.arange(S))
    decay = GAMMA ** np.abs(idx[None, :] - idx[:, None])
    scores = (mxq(f64(q), 2, "e4m3") @ mxq(f64(k), 2, "e4m3").transpose(0, 2, 1)) * decay
    g = scores * sigmoid(scores)
    v = mxq(f64(x), 2, "e4m3") @ unpack_weight(w_v_words, w_v_scales, "e4m3")
    return mxq(g, 2, "e4m3") @ mxq(v, 1, "e4m3")

@@ -1,0 +1,200 @@
+import math
+from contextlib import ExitStack
+
+import concourse.mybir as mybir
+from concourse.masks import make_identity
+
+F32 = mybir.dt.float32
+BF16 = mybir.dt.bfloat16
+I32 = mybir.dt.int32
+U32 = mybir.dt.uint32
+U8 = mybir.dt.uint8
+FP8X4 = mybir.dt.float8_e4m3fn_x4
+MULT = mybir.AluOpType.mult
+MAX = mybir.AluOpType.max
+ACT = mybir.ActivationFunctionType
+
+B, S, H = 4, 1024, 512
+GAMMA = 0.96875
+
+P = 128
+PACK = 4
+K_PASS = P * PACK
+BANK = 512
+ROW_TILES = S // P
+KEY_PASSES = S // K_PASS
+QUERY_HALVES = S // BANK
+
+CENTRE = K_PASS * (KEY_PASSES - 1) + PACK - 1
+DECAY_COLS = CENTRE + S
+
+FLOPS = 2 * B * S * H * (H + 2 * S)
+
+
+def tile_simpleretention_pa_t_kernel(tc, q, k, x, w_v_words, w_v_scales, out):
+    nc = tc.nc
+    with ExitStack() as ctx:
+        const = ctx.enter_context(tc.tile_pool(name="const", bufs=1))
+        raw = ctx.enter_context(tc.tile_pool(name="raw", bufs=B))
+        stage = ctx.enter_context(tc.tile_pool(name="stage", bufs=2))
+        operands = ctx.enter_context(tc.tile_pool(name="operands", bufs=2))
+        prep_psum = ctx.enter_context(tc.psum_pool(name="prep_psum", bufs=3))
+        score_psum = ctx.enter_context(tc.psum_pool(name="score_psum", bufs=3))
+        out_psum = ctx.enter_context(tc.psum_pool(name="out_psum", bufs=2))
+
+        def load_by_word(src, name):
+            rows = raw.tile([P, ROW_TILES, H], BF16, name=name)
+            nc.sync.dma_start(
+                out=rows[:].rearrange("p (c t) f -> p c t f", t=PACK),
+                in_=src.rearrange("(c p t) f -> p c t f", p=P, t=PACK),
+            )
+            return rows
+
+        def load_in_order(src, name):
+            rows = raw.tile([P, ROW_TILES, H], BF16, name=name)
+            nc.sync.dma_start(out=rows[:], in_=src.rearrange("(j p) f -> p j f", p=P))
+            return rows
+
+        x_rows = [load_by_word(x[0], "x_rows")]
+
+        w_codes = const.tile([P, H], U32, align_bytes=64)
+        nc.sync.dma_start(
+            out=w_codes[:].bitcast(I32),
+            in_=w_v_words[0].rearrange("p j t -> p (j t)").bitcast(I32),
+        )
+        w_scales = const.tile([P, H], U8, align_bytes=64)
+        nc.vector.memset(w_scales[:].bitcast(I32), 0)
+        for quadrant in range(4):
+            nc.sync.dma_start(
+                out=w_scales[32 * quadrant : 32 * quadrant + 4, :].bitcast(I32),
+                in_=w_v_scales[0, 4 * quadrant : 4 * quadrant + 4, :].bitcast(I32),
+            )
+
+        k_rows = [load_by_word(k[0], "k_rows")]
+        q_rows = [load_in_order(q[0], "q_rows")]
+        for b in range(1, B):
+            x_rows.append(load_by_word(x[b], "x_rows"))
+            k_rows.append(load_by_word(k[b], "k_rows"))
+            q_rows.append(load_in_order(q[b], "q_rows"))
+
+        identity = const.tile([P, P], F32)
+        make_identity(nc, identity[:])
+
+        distance = const.tile([P, DECAY_COLS], I32)
+        nc.gpsimd.iota(distance[:], pattern=[[1, DECAY_COLS]], base=-CENTRE, channel_multiplier=-PACK)
+        decay_table = const.tile([P, DECAY_COLS], F32)
+        nc.vector.scalar_tensor_tensor(
+            out=decay_table[:], in0=distance[:], scalar=-1.0, in1=distance[:], op0=MULT, op1=MAX
+        )
+        nc.scalar.activation(out=decay_table[:], in_=decay_table[:], func=ACT.Exp, scale=math.log(GAMMA))
+
+        def transpose_and_quantise(rows, name):
+            words = rows[:].bitcast(F32)
+            grouped = stage.tile([P, S * PACK], BF16, align_bytes=64, tag="grouped")
+            grouped_words = grouped[:].bitcast(F32).rearrange("p (j r u) -> p j r u", r=P, u=2)
+            for pair in range(ROW_TILES // 2):
+                bank = prep_psum.tile([P, 2, 2, P], F32, tag="bank")
+                for j in range(2):
+                    for u in range(2):
+                        nc.tensor.transpose(bank[:, j, u, :], words[:, 2 * pair + j, u : H // 2 : 2], identity[:])
+                nc.scalar.copy(
+                    out=grouped_words[:, 2 * pair : 2 * pair + 2],
+                    in_=bank[:].rearrange("p j u r -> p j r u"),
+                )
+            codes = operands.tile([P, S], U32, align_bytes=64, name=name + "_codes")
+            scales = operands.tile([P, S], U8, align_bytes=64, name=name + "_scales")
+            nc.vector.quantize_mx(out=codes[:].bitcast(FP8X4), scales=scales[:], in_=grouped[:])
+            return codes, scales
+
+        def project_values(x_codes, x_scales):
+            v_grouped = stage.tile([P, KEY_PASSES, H, PACK], BF16, align_bytes=64, bufs=1)
+            v_codes = operands.tile([P, KEY_PASSES, H], U32, align_bytes=64)
+            v_scales = operands.tile([P, KEY_PASSES, H], U8, align_bytes=64)
+            for c in range(KEY_PASSES):
+                for piece in range(H // P):
+                    cols = slice(piece * P, (piece + 1) * P)
+                    bank = prep_psum.tile([P, PACK, P], F32, tag="bank")
+                    for t in range(PACK):
+                        tokens = slice((c * PACK + t) * P, (c * PACK + t + 1) * P)
+                        nc.tensor.matmul_mx(
+                            out=bank[:, t, :],
+                            lhsT=x_codes[:, tokens].bitcast(FP8X4),
+                            lhsT_scale=x_scales[:, tokens],
+                            rhs=w_codes[:, cols].bitcast(FP8X4),
+                            rhs_scale=w_scales[:, cols],
+                            start=True,
+                            stop=True,
+                        )
+                    nc.vector.tensor_copy(out=v_grouped[:, c, cols, :], in_=bank[:].rearrange("p t h -> p h t"))
+                nc.vector.quantize_mx(
+                    out=v_codes[:, c, :].bitcast(FP8X4),
+                    scales=v_scales[:, c, :],
+                    in_=v_grouped[:, c].rearrange("p h t -> p (h t)"),
+                )
+            return v_codes, v_scales
+
+        def prepare(b):
+            x_codes, x_scales = transpose_and_quantise(x_rows[b], "x")
+            k_operand = transpose_and_quantise(k_rows[b], "k")
+            q_operand = transpose_and_quantise(q_rows[b], "q")
+            return k_operand, q_operand, project_values(x_codes, x_scales)
+
+        def attend(b, k_operand, q_operand, v_operand):
+            k_codes, k_scales = k_operand
+            q_codes, q_scales = q_operand
+            v_codes, v_scales = v_operand
+            for half in range(QUERY_HALVES):
+                queries = slice(half * BANK, (half + 1) * BANK)
+                g_codes = operands.tile([P, KEY_PASSES, BANK], U32, align_bytes=64)
+                g_scales = operands.tile([P, KEY_PASSES, BANK], U8, align_bytes=64)
+                for c in range(KEY_PASSES):
+                    decayed = stage.tile([P, PACK, BANK], F32)
+                    for t in range(PACK):
+                        keys = slice((c * PACK + t) * P, (c * PACK + t + 1) * P)
+                        scores = score_psum.tile([P, BANK], F32)
+                        nc.tensor.matmul_mx(
+                            out=scores[:],
+                            lhsT=k_codes[:, keys].bitcast(FP8X4),
+                            lhsT_scale=k_scales[:, keys],
+                            rhs=q_codes[:, queries].bitcast(FP8X4),
+                            rhs_scale=q_scales[:, queries],
+                            start=True,
+                            stop=True,
+                        )
+                        first = CENTRE + BANK * half - K_PASS * c - t
+                        nc.vector.tensor_tensor(
+                            out=decayed[:, t, :], in0=scores[:], in1=decay_table[:, first : first + BANK], op=MULT
+                        )
+                    gated = stage.tile([P, BANK, PACK], BF16, align_bytes=64)
+                    nc.scalar.activation(
+                        out=gated[:].rearrange("p (s i) t -> p s t i", i=4),
+                        in_=decayed[:].rearrange("p t (s i) -> p s t i", i=4),
+                        func=ACT.Silu,
+                    )
+                    nc.vector.quantize_mx(
+                        out=g_codes[:, c, :].bitcast(FP8X4),
+                        scales=g_scales[:, c, :],
+                        in_=gated[:].rearrange("p m t -> p (m t)"),
+                    )
+                result = stage.tile([P, BANK // P, H], F32)
+                for j in range(BANK // P):
+                    query_tile = slice(j * P, (j + 1) * P)
+                    acc = out_psum.tile([P, H], F32)
+                    for c in range(KEY_PASSES):
+                        nc.tensor.matmul_mx(
+                            out=acc[:],
+                            lhsT=g_codes[:, c, query_tile].bitcast(FP8X4),
+                            lhsT_scale=g_scales[:, c, query_tile],
+                            rhs=v_codes[:, c, :].bitcast(FP8X4),
+                            rhs_scale=v_scales[:, c, :],
+                            start=(c == 0),
+                            stop=(c == KEY_PASSES - 1),
+                        )
+                    nc.scalar.copy(out=result[:, j, :], in_=acc[:])
+                nc.sync.dma_start(out=out[b, queries, :].rearrange("(j p) h -> p j h", p=P), in_=result[:])
+
+        ready = prepare(0)
+        for b in range(B):
+            following = prepare(b + 1) if b + 1 < B else None
+            attend(b, *ready)
+            ready = following

@@ -10,6 +10,7 @@ I32 = mybir.dt.int32
 U32 = mybir.dt.uint32
 U8 = mybir.dt.uint8
 FP8X4 = mybir.dt.float8_e4m3fn_x4
+ADD = mybir.AluOpType.add
 MULT = mybir.AluOpType.mult
 MAX = mybir.AluOpType.max
 ACT = mybir.ActivationFunctionType
@@ -19,103 +20,115 @@ GAMMA = 0.96875
 
 P = 128
 PACK = 4
-K_PASS = P * PACK
 BANK = 512
-ROW_TILES = S // P
-KEY_PASSES = S // K_PASS
-QUERY_HALVES = S // BANK
+HALVES = S // BANK
+TILES = BANK // P
 
-CENTRE = K_PASS * (KEY_PASSES - 1) + PACK - 1
-DECAY_COLS = CENTRE + S
+IN_ORDER = "(h j p) f -> p h j f"
+BY_WORD = "(h p j) f -> p h j f"
+ROW_ORDER = {"q": IN_ORDER, "k": BY_WORD, "x": BY_WORD}
+
+SOURCES = (("k", 0), ("q", 0), ("k", 1), ("q", 1), ("x", 0), ("x", 1))
+TRANSPOSE_STEPS = 2 * len(SOURCES)
+STEPS = TRANSPOSE_STEPS + HALVES * (H // P)
+
+UNITS = B * HALVES * HALVES
+OUT_TILES = B * S // P
+STEPS_PER_ROUND = B * STEPS // UNITS
+OUT_TILES_PER_ROUND = OUT_TILES // UNITS
+LEAD = 6
+OUT_LAG = 3
 
 FLOPS = 2 * B * S * H * (H + 2 * S)
 
 
 def tile_simpleretention_pa_t_kernel(tc, q, k, x, w_v_words, w_v_scales, out):
     nc = tc.nc
+    inputs = {"q": q, "k": k, "x": x}
     with ExitStack() as ctx:
+        ctx.enter_context(tc.manual_schedule())
         const = ctx.enter_context(tc.tile_pool(name="const", bufs=1))
         raw = ctx.enter_context(tc.tile_pool(name="raw", bufs=B))
         stage = ctx.enter_context(tc.tile_pool(name="stage", bufs=2))
         operands = ctx.enter_context(tc.tile_pool(name="operands", bufs=2))
-        prep_psum = ctx.enter_context(tc.psum_pool(name="prep_psum", bufs=3))
-        score_psum = ctx.enter_context(tc.psum_pool(name="score_psum", bufs=3))
-        out_psum = ctx.enter_context(tc.psum_pool(name="out_psum", bufs=2))
+        psum = ctx.enter_context(tc.psum_pool(name="psum", bufs=8))
 
-        def load_by_word(src, name):
-            rows = raw.tile([P, ROW_TILES, H], BF16, name=name)
-            nc.sync.dma_start(
-                out=rows[:].rearrange("p (c t) f -> p c t f", t=PACK),
-                in_=src.rearrange("(c p t) f -> p c t f", p=P, t=PACK),
-            )
-            return rows
+        width = BANK + PACK - 1
+        offset = const.tile([P, width], I32)
+        nc.gpsimd.iota(offset[:], pattern=[[1, width]], base=1 - PACK, channel_multiplier=-PACK)
+        identity = const.tile([P, P], F32)
+        make_identity(nc, identity[:])
 
-        def load_in_order(src, name):
-            rows = raw.tile([P, ROW_TILES, H], BF16, name=name)
-            nc.sync.dma_start(out=rows[:], in_=src.rearrange("(j p) f -> p j f", p=P))
-            return rows
+        w_scales = const.tile([P, H], U8, align_bytes=64)
+        nc.vector.memset(w_scales[:].bitcast(I32), 0)
 
-        x_rows = [load_by_word(x[0], "x_rows")]
+        rows = {}
 
+        def load_sequence(b):
+            for name in ("k", "q", "x"):
+                rows_tile = raw.tile([P, HALVES, TILES, H], BF16, name=name + "_rows")
+                rows[(name, b)] = rows_tile
+            for name, half in SOURCES:
+                view = inputs[name][b].rearrange(ROW_ORDER[name], p=P, j=TILES)
+                for part in range(2):
+                    pair = slice(2 * part, 2 * part + 2)
+                    nc.sync.dma_start(out=rows[(name, b)][:, half, pair, :], in_=view[:, half, pair, :])
+
+        load_sequence(0)
         w_codes = const.tile([P, H], U32, align_bytes=64)
         nc.sync.dma_start(
             out=w_codes[:].bitcast(I32),
             in_=w_v_words[0].rearrange("p j t -> p (j t)").bitcast(I32),
         )
-        w_scales = const.tile([P, H], U8, align_bytes=64)
-        nc.vector.memset(w_scales[:].bitcast(I32), 0)
         for quadrant in range(4):
             nc.sync.dma_start(
                 out=w_scales[32 * quadrant : 32 * quadrant + 4, :].bitcast(I32),
                 in_=w_v_scales[0, 4 * quadrant : 4 * quadrant + 4, :].bitcast(I32),
             )
-
-        k_rows = [load_by_word(k[0], "k_rows")]
-        q_rows = [load_in_order(q[0], "q_rows")]
         for b in range(1, B):
-            x_rows.append(load_by_word(x[b], "x_rows"))
-            k_rows.append(load_by_word(k[b], "k_rows"))
-            q_rows.append(load_in_order(q[b], "q_rows"))
+            load_sequence(b)
 
-        identity = const.tile([P, P], F32)
-        make_identity(nc, identity[:])
+        decay = const.tile([P, 2 * HALVES - 1, width], F32)
+        shifted = const.tile([P, width], F32)
+        for w in range(2 * HALVES - 1):
+            nc.vector.tensor_scalar(
+                out=shifted[:], in0=offset[:], scalar1=float(BANK * (w - HALVES + 1)), scalar2=None, op0=ADD
+            )
+            nc.vector.scalar_tensor_tensor(
+                out=decay[:, w, :], in0=shifted[:], scalar=-1.0, in1=shifted[:], op0=MULT, op1=MAX
+            )
+        nc.scalar.activation(out=decay[:], in_=decay[:], func=ACT.Exp, scale=math.log(GAMMA))
+        table_warmer = const.tile([P, 1], F32)
+        nc.scalar.activation(out=table_warmer[:], in_=decay[:, 0, 0:1], func=ACT.Silu)
 
-        distance = const.tile([P, DECAY_COLS], I32)
-        nc.gpsimd.iota(distance[:], pattern=[[1, DECAY_COLS]], base=-CENTRE, channel_multiplier=-PACK)
-        decay_table = const.tile([P, DECAY_COLS], F32)
-        nc.vector.scalar_tensor_tensor(
-            out=decay_table[:], in0=distance[:], scalar=-1.0, in1=distance[:], op0=MULT, op1=MAX
-        )
-        nc.scalar.activation(out=decay_table[:], in_=decay_table[:], func=ACT.Exp, scale=math.log(GAMMA))
+        operand = {}
+        in_progress = {}
 
-        def transpose_and_quantise(rows, name):
-            words = rows[:].bitcast(F32)
-            grouped = stage.tile([P, S * PACK], BF16, align_bytes=64, tag="grouped")
-            grouped_words = grouped[:].bitcast(F32).rearrange("p (j r u) -> p j r u", r=P, u=2)
-            for pair in range(ROW_TILES // 2):
-                bank = prep_psum.tile([P, 2, 2, P], F32, tag="bank")
-                for j in range(2):
-                    for u in range(2):
-                        nc.tensor.transpose(bank[:, j, u, :], words[:, 2 * pair + j, u : H // 2 : 2], identity[:])
-                nc.scalar.copy(
-                    out=grouped_words[:, 2 * pair : 2 * pair + 2],
-                    in_=bank[:].rearrange("p j u r -> p j r u"),
-                )
-            codes = operands.tile([P, S], U32, align_bytes=64, name=name + "_codes")
-            scales = operands.tile([P, S], U8, align_bytes=64, name=name + "_scales")
-            nc.vector.quantize_mx(out=codes[:].bitcast(FP8X4), scales=scales[:], in_=grouped[:])
-            return codes, scales
+        def prepare(first, count):
+            completed = []
+            for n in range(first, min(first + count, B * STEPS)):
+                b, step = divmod(n, STEPS)
+                if step < TRANSPOSE_STEPS:
+                    name, half = SOURCES[step // 2]
+                    part, parts = step % 2, 2
+                else:
+                    name, half = "v", (step - TRANSPOSE_STEPS) // (H // P)
+                    part, parts = (step - TRANSPOSE_STEPS) % (H // P), H // P
+                if half == 0 and part == 0:
+                    codes = operands.tile([P, S], U32, align_bytes=64, name=name + "_codes")
+                    scales = operands.tile([P, S], U8, align_bytes=64, name=name + "_scales")
+                    operand[(name, b)] = (codes, scales)
+                if part == 0:
+                    grouped = stage.tile([P, BANK * PACK], BF16, align_bytes=64, bufs=4)
+                    in_progress["grouped"] = grouped
+                grouped = in_progress["grouped"]
 
-        def project_values(x_codes, x_scales):
-            v_grouped = stage.tile([P, KEY_PASSES, H, PACK], BF16, align_bytes=64, bufs=1)
-            v_codes = operands.tile([P, KEY_PASSES, H], U32, align_bytes=64)
-            v_scales = operands.tile([P, KEY_PASSES, H], U8, align_bytes=64)
-            for c in range(KEY_PASSES):
-                for piece in range(H // P):
-                    cols = slice(piece * P, (piece + 1) * P)
-                    bank = prep_psum.tile([P, PACK, P], F32, tag="bank")
+                bank = psum.tile([P, 4, P], F32, tag="bank")
+                if name == "v":
+                    x_codes, x_scales = operand[("x", b)]
+                    cols = slice(part * P, (part + 1) * P)
                     for t in range(PACK):
-                        tokens = slice((c * PACK + t) * P, (c * PACK + t + 1) * P)
+                        tokens = slice((half * TILES + t) * P, (half * TILES + t + 1) * P)
                         nc.tensor.matmul_mx(
                             out=bank[:, t, :],
                             lhsT=x_codes[:, tokens].bitcast(FP8X4),
@@ -125,76 +138,130 @@ def tile_simpleretention_pa_t_kernel(tc, q, k, x, w_v_words, w_v_scales, out):
                             start=True,
                             stop=True,
                         )
-                    nc.vector.tensor_copy(out=v_grouped[:, c, cols, :], in_=bank[:].rearrange("p t h -> p h t"))
-                nc.vector.quantize_mx(
-                    out=v_codes[:, c, :].bitcast(FP8X4),
-                    scales=v_scales[:, c, :],
-                    in_=v_grouped[:, c].rearrange("p h t -> p (h t)"),
+                    source = bank[:].rearrange("p t h -> p h t")
+                    target = grouped[:].rearrange("p (h t) -> p h t", t=PACK)[:, cols, :]
+                else:
+                    words = rows[(name, b)][:, half].bitcast(F32)
+                    for j in range(2):
+                        for u in range(2):
+                            word_cols = slice(u, H // 2, 2) if name == "x" else slice(u * P, (u + 1) * P)
+                            nc.tensor.transpose(bank[:, 2 * j + u, :], words[:, 2 * part + j, word_cols], identity[:])
+                    source = bank[:].rearrange("p (j u) r -> p j r u", u=2)
+                    target = grouped[:].bitcast(F32).rearrange("p (j r u) -> p j r u", r=P, u=2)
+                    target = target[:, 2 * part : 2 * part + 2]
+                if n % STEPS_PER_ROUND == 2 or n < LEAD:
+                    nc.vector.tensor_copy(out=target, in_=source)
+                else:
+                    nc.scalar.copy(out=target, in_=source)
+                if part == parts - 1:
+                    completed.append((name, b, half, grouped))
+            return completed
+
+        def quantise(completed):
+            for name, b, half, grouped in completed:
+                codes, scales = operand[(name, b)]
+                cols = slice(half * BANK, (half + 1) * BANK)
+                nc.vector.quantize_mx(out=codes[:, cols].bitcast(FP8X4), scales=scales[:, cols], in_=grouped[:])
+
+        def unit_of(u):
+            b, rest = divmod(u, HALVES * HALVES)
+            query_half, key_half = divmod(rest, HALVES)
+            return b, query_half, key_half
+
+        def score_passes(u):
+            b, query_half, key_half = unit_of(u)
+            k_codes, k_scales = operand[("k", b)]
+            q_codes, q_scales = operand[("q", b)]
+            queries = slice(query_half * BANK, (query_half + 1) * BANK)
+            banks = []
+            for t in range(PACK):
+                keys = slice((key_half * TILES + t) * P, (key_half * TILES + t + 1) * P)
+                scores = psum.tile([P, BANK], F32, tag="bank")
+                nc.tensor.matmul_mx(
+                    out=scores[:],
+                    lhsT=k_codes[:, keys].bitcast(FP8X4),
+                    lhsT_scale=k_scales[:, keys],
+                    rhs=q_codes[:, queries].bitcast(FP8X4),
+                    rhs_scale=q_scales[:, queries],
+                    start=True,
+                    stop=True,
                 )
-            return v_codes, v_scales
+                banks.append(scores)
+            return banks
 
-        def prepare(b):
-            x_codes, x_scales = transpose_and_quantise(x_rows[b], "x")
-            k_operand = transpose_and_quantise(k_rows[b], "k")
-            q_operand = transpose_and_quantise(q_rows[b], "q")
-            return k_operand, q_operand, project_values(x_codes, x_scales)
+        def apply_decay(u, banks):
+            b, query_half, key_half = unit_of(u)
+            w = query_half - key_half + HALVES - 1
+            decayed = stage.tile([P, PACK, BANK], F32)
+            for t in range(PACK):
+                first = PACK - 1 - t
+                nc.vector.tensor_tensor(
+                    out=decayed[:, t, :], in0=banks[t][:], in1=decay[:, w, first : first + BANK], op=MULT
+                )
+            return decayed
 
-        def attend(b, k_operand, q_operand, v_operand):
-            k_codes, k_scales = k_operand
-            q_codes, q_scales = q_operand
-            v_codes, v_scales = v_operand
-            for half in range(QUERY_HALVES):
-                queries = slice(half * BANK, (half + 1) * BANK)
-                g_codes = operands.tile([P, KEY_PASSES, BANK], U32, align_bytes=64)
-                g_scales = operands.tile([P, KEY_PASSES, BANK], U8, align_bytes=64)
-                for c in range(KEY_PASSES):
-                    decayed = stage.tile([P, PACK, BANK], F32)
-                    for t in range(PACK):
-                        keys = slice((c * PACK + t) * P, (c * PACK + t + 1) * P)
-                        scores = score_psum.tile([P, BANK], F32)
-                        nc.tensor.matmul_mx(
-                            out=scores[:],
-                            lhsT=k_codes[:, keys].bitcast(FP8X4),
-                            lhsT_scale=k_scales[:, keys],
-                            rhs=q_codes[:, queries].bitcast(FP8X4),
-                            rhs_scale=q_scales[:, queries],
-                            start=True,
-                            stop=True,
-                        )
-                        first = CENTRE + BANK * half - K_PASS * c - t
-                        nc.vector.tensor_tensor(
-                            out=decayed[:, t, :], in0=scores[:], in1=decay_table[:, first : first + BANK], op=MULT
-                        )
-                    gated = stage.tile([P, BANK, PACK], BF16, align_bytes=64)
-                    nc.scalar.activation(
-                        out=gated[:].rearrange("p (s i) t -> p s t i", i=4),
-                        in_=decayed[:].rearrange("p t (s i) -> p s t i", i=4),
-                        func=ACT.Silu,
-                    )
-                    nc.vector.quantize_mx(
-                        out=g_codes[:, c, :].bitcast(FP8X4),
-                        scales=g_scales[:, c, :],
-                        in_=gated[:].rearrange("p m t -> p (m t)"),
-                    )
-                result = stage.tile([P, BANK // P, H], F32)
-                for j in range(BANK // P):
-                    query_tile = slice(j * P, (j + 1) * P)
-                    acc = out_psum.tile([P, H], F32)
-                    for c in range(KEY_PASSES):
-                        nc.tensor.matmul_mx(
-                            out=acc[:],
-                            lhsT=g_codes[:, c, query_tile].bitcast(FP8X4),
-                            lhsT_scale=g_scales[:, c, query_tile],
-                            rhs=v_codes[:, c, :].bitcast(FP8X4),
-                            rhs_scale=v_scales[:, c, :],
-                            start=(c == 0),
-                            stop=(c == KEY_PASSES - 1),
-                        )
-                    nc.scalar.copy(out=result[:, j, :], in_=acc[:])
-                nc.sync.dma_start(out=out[b, queries, :].rearrange("(j p) h -> p j h", p=P), in_=result[:])
+        def swish(decayed):
+            gated = stage.tile([P, BANK, PACK], BF16, align_bytes=64)
+            nc.scalar.activation(
+                out=gated[:].rearrange("p (s i) t -> p s t i", i=4),
+                in_=decayed[:].rearrange("p t (s i) -> p s t i", i=4),
+                func=ACT.Silu,
+            )
+            return gated
 
-        ready = prepare(0)
-        for b in range(B):
-            following = prepare(b + 1) if b + 1 < B else None
-            attend(b, *ready)
-            ready = following
+        gates = {}
+
+        def quantise_gates(u, gated):
+            b, query_half, key_half = unit_of(u)
+            if key_half == 0:
+                g_codes = operands.tile([P, HALVES, BANK], U32, align_bytes=64, bufs=3)
+                g_scales = operands.tile([P, HALVES, BANK], U8, align_bytes=64, bufs=3)
+                gates[(b, query_half)] = (g_codes, g_scales)
+            g_codes, g_scales = gates[(b, query_half)]
+            nc.vector.quantize_mx(
+                out=g_codes[:, key_half, :].bitcast(FP8X4),
+                scales=g_scales[:, key_half, :],
+                in_=gated[:].rearrange("p m t -> p (m t)"),
+            )
+
+        def out_tile(o):
+            b, tile_in_sequence = divmod(o, S // P)
+            query_half, j = divmod(tile_in_sequence, TILES)
+            g_codes, g_scales = gates[(b, query_half)]
+            v_codes, v_scales = operand[("v", b)]
+            queries = slice(j * P, (j + 1) * P)
+            acc = psum.tile([P, H], F32, tag="bank")
+            for key_half in range(HALVES):
+                tokens = slice(key_half * BANK, (key_half + 1) * BANK)
+                nc.tensor.matmul_mx(
+                    out=acc[:],
+                    lhsT=g_codes[:, key_half, queries].bitcast(FP8X4),
+                    lhsT_scale=g_scales[:, key_half, queries],
+                    rhs=v_codes[:, tokens].bitcast(FP8X4),
+                    rhs_scale=v_scales[:, tokens],
+                    start=(key_half == 0),
+                    stop=(key_half == HALVES - 1),
+                )
+            result = stage.tile([P, H], F32, bufs=4)
+            if o % 2 == 0:
+                nc.scalar.copy(out=result[:], in_=acc[:])
+            else:
+                nc.vector.tensor_copy(out=result[:], in_=acc[:])
+            nc.sync.dma_start(out=out[b, tile_in_sequence * P : (tile_in_sequence + 1) * P, :], in_=result[:])
+
+        quantise(prepare(0, LEAD))
+        banks = score_passes(0)
+        decayed = None
+        for r in range(UNITS + OUT_LAG):
+            gated = swish(decayed) if 1 <= r <= UNITS else None
+            if r < UNITS:
+                decayed = apply_decay(r, banks)
+            if 1 <= r <= UNITS:
+                quantise_gates(r - 1, gated)
+            completed = prepare(LEAD + STEPS_PER_ROUND * r, STEPS_PER_ROUND)
+            for o in range(OUT_TILES_PER_ROUND * (r - OUT_LAG), OUT_TILES_PER_ROUND * (r - OUT_LAG + 1)):
+                if o >= 0:
+                    out_tile(o)
+            quantise(completed)
+            if r + 1 < UNITS:
+                banks = score_passes(r + 1)

@@ -36,7 +36,7 @@ UNITS = B * HALVES * HALVES
 OUT_TILES = B * S // P
 STEPS_PER_ROUND = B * STEPS // UNITS
 OUT_TILES_PER_ROUND = OUT_TILES // UNITS
-LEAD = 6
+FIRST_STEPS = 5
 OUT_LAG = 3
 
 FLOPS = 2 * B * S * H * (H + 2 * S)
@@ -103,6 +103,7 @@ def tile_simpleretention_pa_t_kernel(tc, q, k, x, w_v_words, w_v_scales, out):
 
         operand = {}
         in_progress = {}
+        quantised = set()
 
         def prepare(first, count):
             completed = []
@@ -125,6 +126,7 @@ def tile_simpleretention_pa_t_kernel(tc, q, k, x, w_v_words, w_v_scales, out):
 
                 bank = psum.tile([P, 4, P], F32, tag="bank")
                 if name == "v":
+                    assert ("x", b, half) in quantised
                     x_codes, x_scales = operand[("x", b)]
                     cols = slice(part * P, (part + 1) * P)
                     for t in range(PACK):
@@ -149,7 +151,7 @@ def tile_simpleretention_pa_t_kernel(tc, q, k, x, w_v_words, w_v_scales, out):
                     source = bank[:].rearrange("p (j u) r -> p j r u", u=2)
                     target = grouped[:].bitcast(F32).rearrange("p (j r u) -> p j r u", r=P, u=2)
                     target = target[:, 2 * part : 2 * part + 2]
-                if n % STEPS_PER_ROUND == 2 or n < LEAD:
+                if n % STEPS_PER_ROUND == 2 or n < FIRST_STEPS:
                     nc.vector.tensor_copy(out=target, in_=source)
                 else:
                     nc.scalar.copy(out=target, in_=source)
@@ -162,6 +164,7 @@ def tile_simpleretention_pa_t_kernel(tc, q, k, x, w_v_words, w_v_scales, out):
                 codes, scales = operand[(name, b)]
                 cols = slice(half * BANK, (half + 1) * BANK)
                 nc.vector.quantize_mx(out=codes[:, cols].bitcast(FP8X4), scales=scales[:, cols], in_=grouped[:])
+                quantised.add((name, b, half))
 
         def unit_of(u):
             b, rest = divmod(u, HALVES * HALVES)
@@ -170,6 +173,7 @@ def tile_simpleretention_pa_t_kernel(tc, q, k, x, w_v_words, w_v_scales, out):
 
         def score_passes(u):
             b, query_half, key_half = unit_of(u)
+            assert ("k", b, key_half) in quantised and ("q", b, query_half) in quantised
             k_codes, k_scales = operand[("k", b)]
             q_codes, q_scales = operand[("q", b)]
             queries = slice(query_half * BANK, (query_half + 1) * BANK)
@@ -232,6 +236,7 @@ def tile_simpleretention_pa_t_kernel(tc, q, k, x, w_v_words, w_v_scales, out):
             queries = slice(j * P, (j + 1) * P)
             acc = psum.tile([P, H], F32, tag="bank")
             for key_half in range(HALVES):
+                assert ("v", b, key_half) in quantised
                 tokens = slice(key_half * BANK, (key_half + 1) * BANK)
                 nc.tensor.matmul_mx(
                     out=acc[:],
@@ -249,16 +254,16 @@ def tile_simpleretention_pa_t_kernel(tc, q, k, x, w_v_words, w_v_scales, out):
                 nc.vector.tensor_copy(out=result[:], in_=acc[:])
             nc.sync.dma_start(out=out[b, tile_in_sequence * P : (tile_in_sequence + 1) * P, :], in_=result[:])
 
-        quantise(prepare(0, LEAD))
-        banks = score_passes(0)
+        quantise(prepare(0, FIRST_STEPS))
+        banks = None
         decayed = None
-        for r in range(UNITS + OUT_LAG):
+        for r in range(-1, UNITS + OUT_LAG):
             gated = swish(decayed) if 1 <= r <= UNITS else None
-            if r < UNITS:
+            if 0 <= r < UNITS:
                 decayed = apply_decay(r, banks)
             if 1 <= r <= UNITS:
                 quantise_gates(r - 1, gated)
-            completed = prepare(LEAD + STEPS_PER_ROUND * r, STEPS_PER_ROUND)
+            completed = prepare(FIRST_STEPS + STEPS_PER_ROUND * (r + 1), STEPS_PER_ROUND)
             for o in range(OUT_TILES_PER_ROUND * (r - OUT_LAG), OUT_TILES_PER_ROUND * (r - OUT_LAG + 1)):
                 if o >= 0:
                     out_tile(o)

@@ -10,9 +10,7 @@ I32 = mybir.dt.int32
 U32 = mybir.dt.uint32
 U8 = mybir.dt.uint8
 FP8X4 = mybir.dt.float8_e4m3fn_x4
-ADD = mybir.AluOpType.add
 MULT = mybir.AluOpType.mult
-MAX = mybir.AluOpType.max
 ACT = mybir.ActivationFunctionType
 
 B, S, H = 4, 1024, 512
@@ -54,8 +52,14 @@ def tile_simpleretention_pa_t_kernel(tc, q, k, x, w_v_words, w_v_scales, out):
         psum = ctx.enter_context(tc.psum_pool(name="psum", bufs=8))
 
         width = BANK + PACK - 1
-        offset = const.tile([P, width], I32)
-        nc.gpsimd.iota(offset[:], pattern=[[1, width]], base=1 - PACK, channel_multiplier=-PACK)
+        offset = const.tile([P, width], F32)
+        nc.gpsimd.iota(
+            offset[:],
+            pattern=[[1, width]],
+            base=1 - PACK,
+            channel_multiplier=-PACK,
+            allow_small_or_imprecise_dtypes=True,
+        )
         identity = const.tile([P, P], F32)
         make_identity(nc, identity[:])
 
@@ -89,13 +93,9 @@ def tile_simpleretention_pa_t_kernel(tc, q, k, x, w_v_words, w_v_scales, out):
             load_sequence(b)
 
         decay = const.tile([P, 2 * HALVES - 1, width], F32)
-        shifted = const.tile([P, width], F32)
         for w in range(2 * HALVES - 1):
-            nc.vector.tensor_scalar(
-                out=shifted[:], in0=offset[:], scalar1=float(BANK * (w - HALVES + 1)), scalar2=None, op0=ADD
-            )
-            nc.vector.scalar_tensor_tensor(
-                out=decay[:, w, :], in0=shifted[:], scalar=-1.0, in1=shifted[:], op0=MULT, op1=MAX
+            nc.scalar.activation(
+                out=decay[:, w, :], in_=offset[:], func=ACT.Abs, bias=float(BANK * (w - HALVES + 1))
             )
         nc.scalar.activation(out=decay[:], in_=decay[:], func=ACT.Exp, scale=math.log(GAMMA))
         table_warmer = const.tile([P, 1], F32)

@@ -44,7 +44,6 @@ def tile_simpleretention_pa_t_kernel(tc, q, k, x, w_v_words, w_v_scales, out):
     nc = tc.nc
     inputs = {"q": q, "k": k, "x": x}
     with ExitStack() as ctx:
-        ctx.enter_context(tc.manual_schedule())
         const = ctx.enter_context(tc.tile_pool(name="const", bufs=1))
         raw = ctx.enter_context(tc.tile_pool(name="raw", bufs=B))
         stage = ctx.enter_context(tc.tile_pool(name="stage", bufs=2))

@@ -247,10 +247,10 @@ def tile_simpleretention_pa_t_kernel(tc, q, k, x, w_v_words, w_v_scales, out):
                     stop=(key_half == HALVES - 1),
                 )
             result = stage.tile([P, H], F32, bufs=4)
-            if o % 2 == 0:
-                nc.scalar.copy(out=result[:], in_=acc[:])
-            else:
+            if o % 4 == 3:
                 nc.vector.tensor_copy(out=result[:], in_=acc[:])
+            else:
+                nc.scalar.copy(out=result[:], in_=acc[:])
             nc.sync.dma_start(out=out[b, tile_in_sequence * P : (tile_in_sequence + 1) * P, :], in_=result[:])
 
         quantise(prepare(0, FIRST_STEPS))

@@ -11,6 +11,7 @@ U32 = mybir.dt.uint32
 U8 = mybir.dt.uint8
 FP8X4 = mybir.dt.float8_e4m3fn_x4
 MULT = mybir.AluOpType.mult
+MIN = mybir.AluOpType.min
 ACT = mybir.ActivationFunctionType
 
 B, S, H = 4, 1024, 512
@@ -26,16 +27,14 @@ IN_ORDER = "(h j p) f -> p h j f"
 BY_WORD = "(h p j) f -> p h j f"
 ROW_ORDER = {"q": IN_ORDER, "k": BY_WORD, "x": BY_WORD}
 
-SOURCES = (("k", 0), ("q", 0), ("k", 1), ("q", 1), ("x", 0), ("x", 1))
-TRANSPOSE_STEPS = 2 * len(SOURCES)
+FIRST_SOURCES = (("k", 0), ("q", 0), ("k", 1), ("x", 0), ("q", 1), ("x", 1))
+LATER_SOURCES = (("k", 0), ("q", 0), ("x", 0), ("x", 1), ("k", 1), ("q", 1))
+TRANSPOSE_STEPS = 2 * len(FIRST_SOURCES)
 STEPS = TRANSPOSE_STEPS + HALVES * (H // P)
 
 UNITS = B * HALVES * HALVES
+TICKS = UNITS * PACK
 OUT_TILES = B * S // P
-STEPS_PER_ROUND = B * STEPS // UNITS
-OUT_TILES_PER_ROUND = OUT_TILES // UNITS
-FIRST_STEPS = 5
-OUT_LAG = 3
 
 FLOPS = 2 * B * S * H * (H + 2 * S)
 
@@ -45,12 +44,16 @@ def tile_simpleretention_pa_t_kernel(tc, q, k, x, w_v_words, w_v_scales, out):
     inputs = {"q": q, "k": k, "x": x}
     with ExitStack() as ctx:
         const = ctx.enter_context(tc.tile_pool(name="const", bufs=1))
-        raw = ctx.enter_context(tc.tile_pool(name="raw", bufs=B))
+        raw = ctx.enter_context(tc.tile_pool(name="raw", bufs=2))
         stage = ctx.enter_context(tc.tile_pool(name="stage", bufs=2))
         operands = ctx.enter_context(tc.tile_pool(name="operands", bufs=2))
         psum = ctx.enter_context(tc.psum_pool(name="psum", bufs=8))
+        ctx.enter_context(tc.manual_schedule())
 
         width = BANK + PACK - 1
+        table_warmer = const.tile([P, 2], F32)
+        nc.vector.memset(table_warmer[:], 0.0)
+        nc.scalar.activation(out=table_warmer[:, 1:2], in_=table_warmer[:, 0:1], func=ACT.Exp)
         offset = const.tile([P, width], F32)
         nc.gpsimd.iota(
             offset[:],
@@ -61,17 +64,19 @@ def tile_simpleretention_pa_t_kernel(tc, q, k, x, w_v_words, w_v_scales, out):
         )
         identity = const.tile([P, P], F32)
         make_identity(nc, identity[:])
-
         w_scales = const.tile([P, H], U8, align_bytes=64)
         nc.vector.memset(w_scales[:].bitcast(I32), 0)
 
         rows = {}
 
+        def sources(b):
+            return FIRST_SOURCES if b == 0 else LATER_SOURCES
+
         def load_sequence(b):
             for name in ("k", "q", "x"):
                 rows_tile = raw.tile([P, HALVES, TILES, H], BF16, name=name + "_rows")
                 rows[(name, b)] = rows_tile
-            for name, half in SOURCES:
+            for name, half in sources(b):
                 view = inputs[name][b].rearrange(ROW_ORDER[name], p=P, j=TILES)
                 for part in range(2):
                     pair = slice(2 * part, 2 * part + 2)
@@ -91,181 +96,262 @@ def tile_simpleretention_pa_t_kernel(tc, q, k, x, w_v_words, w_v_scales, out):
         for b in range(1, B):
             load_sequence(b)
 
+        log_gamma = math.log(GAMMA)
+        rising = const.tile([P, width], F32)
+        falling = const.tile([P, width], F32)
+        nc.scalar.activation(out=falling[:], in_=offset[:], func=ACT.Exp, scale=log_gamma)
+        nc.scalar.activation(out=rising[:], in_=offset[:], func=ACT.Exp, scale=-log_gamma)
+        nc.scalar.activation(out=table_warmer[:, 1:2], in_=table_warmer[:, 0:1], func=ACT.Silu)
         decay = const.tile([P, 2 * HALVES - 1, width], F32)
-        for w in range(2 * HALVES - 1):
-            nc.scalar.activation(
-                out=decay[:, w, :], in_=offset[:], func=ACT.Abs, bias=float(BANK * (w - HALVES + 1))
-            )
-        nc.scalar.activation(out=decay[:], in_=decay[:], func=ACT.Exp, scale=math.log(GAMMA))
-        table_warmer = const.tile([P, 1], F32)
-        nc.scalar.activation(out=table_warmer[:], in_=decay[:, 0, 0:1], func=ACT.Silu)
+
+        def make_decay(w):
+            if w == 1:
+                nc.vector.tensor_tensor(out=decay[:, w, :], in0=falling[:], in1=rising[:], op=MIN)
+            else:
+                near = rising if w == 0 else falling
+                nc.vector.tensor_scalar_mul(out=decay[:, w, :], in0=near[:], scalar1=GAMMA**BANK)
 
         operand = {}
         in_progress = {}
         quantised = set()
+        completed = []
 
-        def prepare(first, count):
-            completed = []
-            for n in range(first, min(first + count, B * STEPS)):
-                b, step = divmod(n, STEPS)
-                if step < TRANSPOSE_STEPS:
-                    name, half = SOURCES[step // 2]
-                    part, parts = step % 2, 2
-                else:
-                    name, half = "v", (step - TRANSPOSE_STEPS) // (H // P)
-                    part, parts = (step - TRANSPOSE_STEPS) % (H // P), H // P
-                if half == 0 and part == 0:
-                    codes = operands.tile([P, S], U32, align_bytes=64, name=name + "_codes")
-                    scales = operands.tile([P, S], U8, align_bytes=64, name=name + "_scales")
-                    operand[(name, b)] = (codes, scales)
-                if part == 0:
-                    grouped = stage.tile([P, BANK * PACK], BF16, align_bytes=64, bufs=4)
-                    in_progress["grouped"] = grouped
-                grouped = in_progress["grouped"]
+        def prepare(n, on_vector):
+            b, step = divmod(n, STEPS)
+            if step < TRANSPOSE_STEPS:
+                name, half = sources(b)[step // 2]
+                part, parts = step % 2, 2
+            else:
+                name, half = "v", (step - TRANSPOSE_STEPS) // (H // P)
+                part, parts = (step - TRANSPOSE_STEPS) % (H // P), H // P
+            if half == 0 and part == 0:
+                codes = operands.tile([P, S], U32, align_bytes=64, name=name + "_codes")
+                scales = operands.tile([P, S], U8, align_bytes=64, name=name + "_scales")
+                operand[(name, b)] = (codes, scales)
+            if part == 0:
+                grouped = stage.tile([P, BANK * PACK], BF16, align_bytes=64, bufs=4)
+                in_progress["grouped"] = grouped
+            grouped = in_progress["grouped"]
 
-                bank = psum.tile([P, 4, P], F32, tag="bank")
-                if name == "v":
-                    assert ("x", b, half) in quantised
-                    x_codes, x_scales = operand[("x", b)]
-                    cols = slice(part * P, (part + 1) * P)
-                    for t in range(PACK):
-                        tokens = slice((half * TILES + t) * P, (half * TILES + t + 1) * P)
-                        nc.tensor.matmul_mx(
-                            out=bank[:, t, :],
-                            lhsT=x_codes[:, tokens].bitcast(FP8X4),
-                            lhsT_scale=x_scales[:, tokens],
-                            rhs=w_codes[:, cols].bitcast(FP8X4),
-                            rhs_scale=w_scales[:, cols],
-                            start=True,
-                            stop=True,
-                        )
-                    source = bank[:].rearrange("p t h -> p h t")
-                    target = grouped[:].rearrange("p (h t) -> p h t", t=PACK)[:, cols, :]
-                else:
-                    words = rows[(name, b)][:, half].bitcast(F32)
-                    for j in range(2):
-                        for u in range(2):
-                            word_cols = slice(u, H // 2, 2) if name == "x" else slice(u * P, (u + 1) * P)
-                            nc.tensor.transpose(bank[:, 2 * j + u, :], words[:, 2 * part + j, word_cols], identity[:])
-                    source = bank[:].rearrange("p (j u) r -> p j r u", u=2)
-                    target = grouped[:].bitcast(F32).rearrange("p (j r u) -> p j r u", r=P, u=2)
-                    target = target[:, 2 * part : 2 * part + 2]
-                if n % STEPS_PER_ROUND == 2 or n < FIRST_STEPS:
-                    nc.vector.tensor_copy(out=target, in_=source)
-                else:
-                    nc.scalar.copy(out=target, in_=source)
-                if part == parts - 1:
-                    completed.append((name, b, half, grouped))
-            return completed
+            bank = psum.tile([P, 4, P], F32, tag="bank")
+            if name == "v":
+                assert ("x", b, half) in quantised
+                x_codes, x_scales = operand[("x", b)]
+                cols = slice(part * P, (part + 1) * P)
+                for t in range(PACK):
+                    tokens = slice((half * TILES + t) * P, (half * TILES + t + 1) * P)
+                    nc.tensor.matmul_mx(
+                        out=bank[:, t, :],
+                        lhsT=x_codes[:, tokens].bitcast(FP8X4),
+                        lhsT_scale=x_scales[:, tokens],
+                        rhs=w_codes[:, cols].bitcast(FP8X4),
+                        rhs_scale=w_scales[:, cols],
+                        start=True,
+                        stop=True,
+                    )
+                source = bank[:].rearrange("p t h -> p h t")
+                target = grouped[:].rearrange("p (h t) -> p h t", t=PACK)[:, cols, :]
+            else:
+                words = rows[(name, b)][:, half].bitcast(F32)
+                for j in range(2):
+                    for u in range(2):
+                        word_cols = slice(u, H // 2, 2) if name == "x" else slice(u * P, (u + 1) * P)
+                        nc.tensor.transpose(bank[:, 2 * j + u, :], words[:, 2 * part + j, word_cols], identity[:])
+                source = bank[:].rearrange("p (j u) r -> p j r u", u=2)
+                target = grouped[:].bitcast(F32).rearrange("p (j r u) -> p j r u", r=P, u=2)
+                target = target[:, 2 * part : 2 * part + 2]
+            if on_vector:
+                nc.vector.tensor_copy(out=target, in_=source)
+            else:
+                nc.scalar.copy(out=target, in_=source)
+            if part == parts - 1:
+                completed.append((name, b, half, grouped))
 
-        def quantise(completed):
-            for name, b, half, grouped in completed:
-                codes, scales = operand[(name, b)]
-                cols = slice(half * BANK, (half + 1) * BANK)
-                nc.vector.quantize_mx(out=codes[:, cols].bitcast(FP8X4), scales=scales[:, cols], in_=grouped[:])
-                quantised.add((name, b, half))
+        def quantise_next():
+            name, b, half, grouped = completed[0]
+            completed.remove(completed[0])
+            codes, scales = operand[(name, b)]
+            cols = slice(half * BANK, (half + 1) * BANK)
+            nc.vector.quantize_mx(out=codes[:, cols].bitcast(FP8X4), scales=scales[:, cols], in_=grouped[:])
+            quantised.add((name, b, half))
 
         def unit_of(u):
             b, rest = divmod(u, HALVES * HALVES)
             query_half, key_half = divmod(rest, HALVES)
             return b, query_half, key_half
 
-        def score_passes(u):
+        score_banks = {}
+
+        def score_pass(k):
+            u, t = divmod(k, PACK)
             b, query_half, key_half = unit_of(u)
             assert ("k", b, key_half) in quantised and ("q", b, query_half) in quantised
             k_codes, k_scales = operand[("k", b)]
             q_codes, q_scales = operand[("q", b)]
             queries = slice(query_half * BANK, (query_half + 1) * BANK)
-            banks = []
-            for t in range(PACK):
-                keys = slice((key_half * TILES + t) * P, (key_half * TILES + t + 1) * P)
-                scores = psum.tile([P, BANK], F32, tag="bank")
-                nc.tensor.matmul_mx(
-                    out=scores[:],
-                    lhsT=k_codes[:, keys].bitcast(FP8X4),
-                    lhsT_scale=k_scales[:, keys],
-                    rhs=q_codes[:, queries].bitcast(FP8X4),
-                    rhs_scale=q_scales[:, queries],
-                    start=True,
-                    stop=True,
-                )
-                banks.append(scores)
-            return banks
+            keys = slice((key_half * TILES + t) * P, (key_half * TILES + t + 1) * P)
+            scores = psum.tile([P, BANK], F32, tag="bank")
+            nc.tensor.matmul_mx(
+                out=scores[:],
+                lhsT=k_codes[:, keys].bitcast(FP8X4),
+                lhsT_scale=k_scales[:, keys],
+                rhs=q_codes[:, queries].bitcast(FP8X4),
+                rhs_scale=q_scales[:, queries],
+                start=True,
+                stop=True,
+            )
+            score_banks[k] = scores
 
-        def apply_decay(u, banks):
+        decayed_of = {}
+
+        def apply_decay(k):
+            u, t = divmod(k, PACK)
             b, query_half, key_half = unit_of(u)
             w = query_half - key_half + HALVES - 1
-            decayed = stage.tile([P, PACK, BANK], F32)
-            for t in range(PACK):
-                first = PACK - 1 - t
-                nc.vector.tensor_tensor(
-                    out=decayed[:, t, :], in0=banks[t][:], in1=decay[:, w, first : first + BANK], op=MULT
-                )
-            return decayed
+            if t == 0:
+                decayed = stage.tile([P, PACK, BANK], F32)
+                decayed_of[u] = decayed
+            first = PACK - 1 - t
+            nc.vector.tensor_tensor(
+                out=decayed_of[u][:, t, :],
+                in0=score_banks[k][:],
+                in1=decay[:, w, first : first + BANK],
+                op=MULT,
+            )
 
-        def swish(decayed):
-            gated = stage.tile([P, BANK, PACK], BF16, align_bytes=64)
+        gated_of = {}
+
+        def swish(u, piece, pieces):
+            if piece == 0:
+                gated = stage.tile([P, BANK, PACK], BF16, align_bytes=64)
+                gated_of[u] = gated
+            queries = slice(piece * BANK // pieces, (piece + 1) * BANK // pieces)
             nc.scalar.activation(
-                out=gated[:].rearrange("p (s i) t -> p s t i", i=4),
-                in_=decayed[:].rearrange("p t (s i) -> p s t i", i=4),
+                out=gated_of[u][:, queries, :].rearrange("p (s i) t -> p s t i", i=4),
+                in_=decayed_of[u][:, :, queries].rearrange("p t (s i) -> p s t i", i=4),
                 func=ACT.Silu,
             )
-            return gated
 
         gates = {}
 
-        def quantise_gates(u, gated):
+        def quantise_gates(u, piece, pieces):
             b, query_half, key_half = unit_of(u)
-            if key_half == 0:
+            if key_half == 0 and piece == 0:
                 g_codes = operands.tile([P, HALVES, BANK], U32, align_bytes=64, bufs=3)
                 g_scales = operands.tile([P, HALVES, BANK], U8, align_bytes=64, bufs=3)
                 gates[(b, query_half)] = (g_codes, g_scales)
             g_codes, g_scales = gates[(b, query_half)]
+            queries = slice(piece * BANK // pieces, (piece + 1) * BANK // pieces)
             nc.vector.quantize_mx(
-                out=g_codes[:, key_half, :].bitcast(FP8X4),
-                scales=g_scales[:, key_half, :],
-                in_=gated[:].rearrange("p m t -> p (m t)"),
+                out=g_codes[:, key_half, queries].bitcast(FP8X4),
+                scales=g_scales[:, key_half, queries],
+                in_=gated_of[u][:, queries, :].rearrange("p m t -> p (m t)"),
             )
 
-        def out_tile(o):
+        out_banks = {}
+
+        def out_pass(o, key_half):
             b, tile_in_sequence = divmod(o, S // P)
             query_half, j = divmod(tile_in_sequence, TILES)
+            assert ("v", b, key_half) in quantised
             g_codes, g_scales = gates[(b, query_half)]
             v_codes, v_scales = operand[("v", b)]
             queries = slice(j * P, (j + 1) * P)
-            acc = psum.tile([P, H], F32, tag="bank")
-            for key_half in range(HALVES):
-                assert ("v", b, key_half) in quantised
-                tokens = slice(key_half * BANK, (key_half + 1) * BANK)
-                nc.tensor.matmul_mx(
-                    out=acc[:],
-                    lhsT=g_codes[:, key_half, queries].bitcast(FP8X4),
-                    lhsT_scale=g_scales[:, key_half, queries],
-                    rhs=v_codes[:, tokens].bitcast(FP8X4),
-                    rhs_scale=v_scales[:, tokens],
-                    start=(key_half == 0),
-                    stop=(key_half == HALVES - 1),
-                )
-            result = stage.tile([P, H], F32, bufs=4)
-            if o % 4 == 3:
-                nc.vector.tensor_copy(out=result[:], in_=acc[:])
+            tokens = slice(key_half * BANK, (key_half + 1) * BANK)
+            if key_half == 0:
+                acc = psum.tile([P, H], F32, tag="bank")
+                out_banks[o] = acc
+            nc.tensor.matmul_mx(
+                out=out_banks[o][:],
+                lhsT=g_codes[:, key_half, queries].bitcast(FP8X4),
+                lhsT_scale=g_scales[:, key_half, queries],
+                rhs=v_codes[:, tokens].bitcast(FP8X4),
+                rhs_scale=v_scales[:, tokens],
+                start=(key_half == 0),
+                stop=(key_half == HALVES - 1),
+            )
+
+        def store_out(o, on_vector):
+            b, tile_in_sequence = divmod(o, S // P)
+            result = stage.tile([P, H], F32, bufs=OUT_TILES)
+            if on_vector:
+                nc.vector.tensor_copy(out=result[:], in_=out_banks[o][:])
             else:
-                nc.scalar.copy(out=result[:], in_=acc[:])
+                nc.scalar.copy(out=result[:], in_=out_banks[o][:])
             nc.sync.dma_start(out=out[b, tile_in_sequence * P : (tile_in_sequence + 1) * P, :], in_=result[:])
 
-        quantise(prepare(0, FIRST_STEPS))
-        banks = None
-        decayed = None
-        for r in range(-1, UNITS + OUT_LAG):
-            gated = swish(decayed) if 1 <= r <= UNITS else None
-            if 0 <= r < UNITS:
-                decayed = apply_decay(r, banks)
-            if 1 <= r <= UNITS:
-                quantise_gates(r - 1, gated)
-            completed = prepare(FIRST_STEPS + STEPS_PER_ROUND * (r + 1), STEPS_PER_ROUND)
-            for o in range(OUT_TILES_PER_ROUND * (r - OUT_LAG), OUT_TILES_PER_ROUND * (r - OUT_LAG + 1)):
-                if o >= 0:
-                    out_tile(o)
-            quantise(completed)
+        def out_tile(o, on_vector):
+            for key_half in range(HALVES):
+                out_pass(o, key_half)
+            store_out(o, on_vector)
+
+        def steps_due(r):
+            return min(12 + 6 * r if r < 3 else 15 + 5 * r, B * STEPS)
+
+        def outs_due(r):
+            if r >= UNITS - 1:
+                return OUT_TILES - TILES - 2
+            return max(0, 2 * (r - 2))
+
+        def on_vector(n):
+            return n % 5 == 0
+
+        def out_on_vector(o):
+            return o % 4 == 3
+
+        for n in range(2):
+            prepare(n, True)
+        prepare(2, True)
+        quantise_next()
+        prepare(3, False)
+        quantise_next()
+        for n in range(4, 6):
+            prepare(n, False)
+        make_decay(1)
+        prepare(6, False)
+        for t in range(PACK):
+            score_pass(t)
+        done = 7
+        outs = 0
+        for r in range(UNITS):
+            if r > 0:
+                swish(r - 1, 0, 1)
+            for t in range(PACK):
+                apply_decay(PACK * r + t)
+                if t % 2 == 1 and completed:
+                    quantise_next()
+            if r == 0:
+                make_decay(0)
+                make_decay(2)
+            else:
+                while completed:
+                    quantise_next()
+            while done < steps_due(r) or outs < outs_due(r):
+                if done < steps_due(r):
+                    prepare(done, on_vector(done))
+                    done += 1
+                if outs < outs_due(r):
+                    out_tile(outs, out_on_vector(outs))
+                    outs += 1
+            if r > 0:
+                quantise_gates(r - 1, 0, 1)
+            else:
+                quantise_next()
             if r + 1 < UNITS:
-                banks = score_passes(r + 1)
+                for t in range(PACK):
+                    score_pass(PACK * (r + 1) + t)
+        last = OUT_TILES - TILES
+        for piece in range(TILES):
+            swish(UNITS - 1, piece, TILES)
+        for o in range(outs, last):
+            out_tile(o, True)
+        for piece in range(TILES):
+            out_pass(last + piece, 0)
+        for piece in range(TILES):
+            quantise_gates(UNITS - 1, piece, TILES)
+            out_pass(last + piece, 1)
+            if piece == 1:
+                store_out(last, True)
+        store_out(last + 1, False)
+        store_out(last + 2, True)
+        store_out(last + 3, False)

@@ -27,7 +27,7 @@ IN_ORDER = "(h j p) f -> p h j f"
 BY_WORD = "(h p j) f -> p h j f"
 ROW_ORDER = {"q": IN_ORDER, "k": BY_WORD, "x": BY_WORD}
 
-FIRST_SOURCES = (("k", 0), ("q", 0), ("k", 1), ("x", 0), ("q", 1), ("x", 1))
+FIRST_SOURCES = (("k", 0), ("q", 0), ("k", 1), ("x", 0), ("x", 1), ("q", 1))
 LATER_SOURCES = (("k", 0), ("q", 0), ("x", 0), ("x", 1), ("k", 1), ("q", 1))
 TRANSPOSE_STEPS = 2 * len(FIRST_SOURCES)
 STEPS = TRANSPOSE_STEPS + HALVES * (H // P)
@@ -297,7 +297,7 @@ def tile_simpleretention_pa_t_kernel(tc, q, k, x, w_v_words, w_v_scales, out):
             return n % 5 == 0
 
         def out_on_vector(o):
-            return o % 4 == 3
+            return o % 3 == 2
 
         for n in range(2):
             prepare(n, True)
@@ -310,8 +310,10 @@ def tile_simpleretention_pa_t_kernel(tc, q, k, x, w_v_words, w_v_scales, out):
         make_decay(1)
         prepare(6, False)
         for t in range(PACK):
+            if t == 2:
+                prepare(7, False)
             score_pass(t)
-        done = 7
+        done = 8
         outs = 0
         for r in range(UNITS):
             if r > 0:

@@ -12,6 +12,7 @@ U8 = mybir.dt.uint8
 FP8X4 = mybir.dt.float8_e4m3fn_x4
 MULT = mybir.AluOpType.mult
 MIN = mybir.AluOpType.min
+ADD = mybir.AluOpType.add
 ACT = mybir.ActivationFunctionType
 
 B, S, H = 4, 1024, 512
@@ -36,6 +37,9 @@ UNITS = B * HALVES * HALVES
 TICKS = UNITS * PACK
 OUT_TILES = B * S // P
 
+WARM_STEPS = 7
+WARM_UP = 4
+
 FLOPS = 2 * B * S * H * (H + 2 * S)
 
 
@@ -54,6 +58,8 @@ def tile_simpleretention_pa_t_kernel(tc, q, k, x, w_v_words, w_v_scales, out):
         table_warmer = const.tile([P, 2], F32)
         nc.vector.memset(table_warmer[:], 0.0)
         nc.scalar.activation(out=table_warmer[:, 1:2], in_=table_warmer[:, 0:1], func=ACT.Exp)
+        zeros = const.tile([P, BANK], BF16)
+        nc.vector.memset(zeros[:].bitcast(I32), 0)
         offset = const.tile([P, width], F32)
         nc.gpsimd.iota(
             offset[:],
@@ -66,6 +72,14 @@ def tile_simpleretention_pa_t_kernel(tc, q, k, x, w_v_words, w_v_scales, out):
         make_identity(nc, identity[:])
         w_scales = const.tile([P, H], U8, align_bytes=64)
         nc.vector.memset(w_scales[:].bitcast(I32), 0)
+
+        warm = psum.tile([P, BANK], F32, tag="bank")
+
+        def keep_warm(columns):
+            nc.tensor.matmul(warm[:, :columns], lhsT=zeros[:, :P], rhs=zeros[:, :columns], start=True, stop=True)
+
+        for i in range(WARM_UP):
+            keep_warm(BANK)
 
         rows = {}
 
@@ -102,14 +116,18 @@ def tile_simpleretention_pa_t_kernel(tc, q, k, x, w_v_words, w_v_scales, out):
         nc.scalar.activation(out=falling[:], in_=offset[:], func=ACT.Exp, scale=log_gamma)
         nc.scalar.activation(out=rising[:], in_=offset[:], func=ACT.Exp, scale=-log_gamma)
         nc.scalar.activation(out=table_warmer[:, 1:2], in_=table_warmer[:, 0:1], func=ACT.Silu)
-        decay = const.tile([P, 2 * HALVES - 1, width], F32)
+        decay = {}
 
         def make_decay(w):
+            table = const.tile([P, width], F32, name="decay_" + str(w))
+            decay[w] = table
             if w == 1:
-                nc.vector.tensor_tensor(out=decay[:, w, :], in0=falling[:], in1=rising[:], op=MIN)
+                nc.vector.tensor_tensor(out=table[:], in0=falling[:], in1=rising[:], op=MIN)
             else:
                 near = rising if w == 0 else falling
-                nc.vector.tensor_scalar_mul(out=decay[:, w, :], in0=near[:], scalar1=GAMMA**BANK)
+                nc.gpsimd.tensor_scalar(
+                    out=table[:], in0=near[:], scalar1=GAMMA**BANK, scalar2=0.0, op0=MULT, op1=ADD
+                )
 
         operand = {}
         in_progress = {}
@@ -152,6 +170,8 @@ def tile_simpleretention_pa_t_kernel(tc, q, k, x, w_v_words, w_v_scales, out):
                 source = bank[:].rearrange("p t h -> p h t")
                 target = grouped[:].rearrange("p (h t) -> p h t", t=PACK)[:, cols, :]
             else:
+                if n < WARM_STEPS:
+                    nc.tensor.matmul(bank[:, 0:3, :], lhsT=zeros[:, :P], rhs=zeros[:, : 3 * P], start=True, stop=True)
                 words = rows[(name, b)][:, half].bitcast(F32)
                 for j in range(2):
                     for u in range(2):
@@ -215,7 +235,7 @@ def tile_simpleretention_pa_t_kernel(tc, q, k, x, w_v_words, w_v_scales, out):
             nc.vector.tensor_tensor(
                 out=decayed_of[u][:, t, :],
                 in0=score_banks[k][:],
-                in1=decay[:, w, first : first + BANK],
+                in1=decay[w][:, first : first + BANK],
                 op=MULT,
             )
 
@@ -299,15 +319,16 @@ def tile_simpleretention_pa_t_kernel(tc, q, k, x, w_v_words, w_v_scales, out):
         def out_on_vector(o):
             return o % 3 == 2
 
-        for n in range(2):
+        for n in range(3):
             prepare(n, True)
-        prepare(2, True)
         quantise_next()
         prepare(3, False)
         quantise_next()
         for n in range(4, 6):
             prepare(n, False)
         make_decay(1)
+        make_decay(0)
+        make_decay(2)
         prepare(6, False)
         for t in range(PACK):
             if t == 2:
@@ -322,17 +343,14 @@ def tile_simpleretention_pa_t_kernel(tc, q, k, x, w_v_words, w_v_scales, out):
                 apply_decay(PACK * r + t)
                 if t % 2 == 1 and completed:
                     quantise_next()
-            if r == 0:
-                make_decay(0)
-                make_decay(2)
-            else:
-                while completed:
-                    quantise_next()
+            while r > 0 and completed:
+                quantise_next()
             while done < steps_due(r) or outs < outs_due(r):
-                if done < steps_due(r):
-                    prepare(done, on_vector(done))
-                    done += 1
-                if outs < outs_due(r):
+                for i in range(2):
+                    if done < steps_due(r):
+                        prepare(done, on_vector(done))
+                        done += 1
+                while outs < outs_due(r):
                     out_tile(outs, out_on_vector(outs))
                     outs += 1
             if r > 0:

@@ -56,7 +56,7 @@ def tile_simpleretention_pa_t_kernel(tc, q, k, x, w_v_words, w_v_scales, out):
 
         width = BANK + PACK - 1
         table_warmer = const.tile([P, 2], F32)
-        nc.vector.memset(table_warmer[:], 0.0)
+        nc.gpsimd.memset(table_warmer[:], 0.0)
         nc.scalar.activation(out=table_warmer[:, 1:2], in_=table_warmer[:, 0:1], func=ACT.Exp)
         zeros = const.tile([P, BANK], BF16)
         nc.vector.memset(zeros[:].bitcast(I32), 0)
@@ -170,7 +170,7 @@ def tile_simpleretention_pa_t_kernel(tc, q, k, x, w_v_words, w_v_scales, out):
                 source = bank[:].rearrange("p t h -> p h t")
                 target = grouped[:].rearrange("p (h t) -> p h t", t=PACK)[:, cols, :]
             else:
-                if n < WARM_STEPS:
+                if 0 < n < WARM_STEPS:
                     nc.tensor.matmul(bank[:, 0:3, :], lhsT=zeros[:, :P], rhs=zeros[:, : 3 * P], start=True, stop=True)
                 words = rows[(name, b)][:, half].bitcast(F32)
                 for j in range(2):

@@ -247,8 +247,8 @@ def tile_simpleretention_pa_t_kernel(tc, q, k, x, w_v_words, w_v_scales, out):
                 gated_of[u] = gated
             queries = slice(piece * BANK // pieces, (piece + 1) * BANK // pieces)
             nc.scalar.activation(
-                out=gated_of[u][:, queries, :].rearrange("p (s i) t -> p s t i", i=4),
-                in_=decayed_of[u][:, :, queries].rearrange("p t (s i) -> p s t i", i=4),
+                out=gated_of[u][:, queries, :].rearrange("p (s i) t -> p s t i", i=2),
+                in_=decayed_of[u][:, :, queries].rearrange("p t (s i) -> p s t i", i=2),
                 func=ACT.Silu,
             )
 

import math
from contextlib import ExitStack

import concourse.mybir as mybir
from concourse.masks import make_identity

F32 = mybir.dt.float32
BF16 = mybir.dt.bfloat16
I32 = mybir.dt.int32
U32 = mybir.dt.uint32
U8 = mybir.dt.uint8
FP8X4 = mybir.dt.float8_e4m3fn_x4
MULT = mybir.AluOpType.mult
MIN = mybir.AluOpType.min
ADD = mybir.AluOpType.add
ACT = mybir.ActivationFunctionType

B, S, H = 4, 1024, 512
GAMMA = 0.96875

P = 128
PACK = 4
BANK = 512
HALVES = S // BANK
TILES = BANK // P

IN_ORDER = "(h j p) f -> p h j f"
BY_WORD = "(h p j) f -> p h j f"
ROW_ORDER = {"q": IN_ORDER, "k": BY_WORD, "x": BY_WORD}

FIRST_SOURCES = (("k", 0), ("q", 0), ("k", 1), ("x", 0), ("x", 1), ("q", 1))
LATER_SOURCES = (("k", 0), ("q", 0), ("x", 0), ("x", 1), ("k", 1), ("q", 1))
TRANSPOSE_STEPS = 2 * len(FIRST_SOURCES)
STEPS = TRANSPOSE_STEPS + HALVES * (H // P)

UNITS = B * HALVES * HALVES
TICKS = UNITS * PACK
OUT_TILES = B * S // P

WARM_STEPS = 7
WARM_UP = 4

FLOPS = 2 * B * S * H * (H + 2 * S)


def tile_simpleretention_pa_t_kernel(tc, q, k, x, w_v_words, w_v_scales, out):
    nc = tc.nc
    inputs = {"q": q, "k": k, "x": x}
    with ExitStack() as ctx:
        const = ctx.enter_context(tc.tile_pool(name="const", bufs=1))
        raw = ctx.enter_context(tc.tile_pool(name="raw", bufs=2))
        stage = ctx.enter_context(tc.tile_pool(name="stage", bufs=2))
        operands = ctx.enter_context(tc.tile_pool(name="operands", bufs=2))
        psum = ctx.enter_context(tc.psum_pool(name="psum", bufs=8))
        ctx.enter_context(tc.manual_schedule())

        width = BANK + PACK - 1
        table_warmer = const.tile([P, 2], F32)
        nc.gpsimd.memset(table_warmer[:], 0.0)
        nc.scalar.activation(out=table_warmer[:, 1:2], in_=table_warmer[:, 0:1], func=ACT.Exp)
        zeros = const.tile([P, BANK], BF16)
        nc.vector.memset(zeros[:].bitcast(I32), 0)
        offset = const.tile([P, width], F32)
        nc.gpsimd.iota(
            offset[:],
            pattern=[[1, width]],
            base=1 - PACK,
            channel_multiplier=-PACK,
            allow_small_or_imprecise_dtypes=True,
        )
        identity = const.tile([P, P], F32)
        make_identity(nc, identity[:])
        w_scales = const.tile([P, H], U8, align_bytes=64)
        nc.vector.memset(w_scales[:].bitcast(I32), 0)

        warm = psum.tile([P, BANK], F32, tag="bank")

        def keep_warm(columns):
            nc.tensor.matmul(warm[:, :columns], lhsT=zeros[:, :P], rhs=zeros[:, :columns], start=True, stop=True)

        for i in range(WARM_UP):
            keep_warm(BANK)

        rows = {}

        def sources(b):
            return FIRST_SOURCES if b == 0 else LATER_SOURCES

        def load_sequence(b):
            for name in ("k", "q", "x"):
                rows_tile = raw.tile([P, HALVES, TILES, H], BF16, name=name + "_rows")
                rows[(name, b)] = rows_tile
            for name, half in sources(b):
                view = inputs[name][b].rearrange(ROW_ORDER[name], p=P, j=TILES)
                for part in range(2):
                    pair = slice(2 * part, 2 * part + 2)
                    nc.sync.dma_start(out=rows[(name, b)][:, half, pair, :], in_=view[:, half, pair, :])

        load_sequence(0)
        w_codes = const.tile([P, H], U32, align_bytes=64)
        nc.sync.dma_start(
            out=w_codes[:].bitcast(I32),
            in_=w_v_words[0].rearrange("p j t -> p (j t)").bitcast(I32),
        )
        for quadrant in range(4):
            nc.sync.dma_start(
                out=w_scales[32 * quadrant : 32 * quadrant + 4, :].bitcast(I32),
                in_=w_v_scales[0, 4 * quadrant : 4 * quadrant + 4, :].bitcast(I32),
            )
        for b in range(1, B):
            load_sequence(b)

        log_gamma = math.log(GAMMA)
        rising = const.tile([P, width], F32)
        falling = const.tile([P, width], F32)
        nc.scalar.activation(out=falling[:], in_=offset[:], func=ACT.Exp, scale=log_gamma)
        nc.scalar.activation(out=rising[:], in_=offset[:], func=ACT.Exp, scale=-log_gamma)
        nc.scalar.activation(out=table_warmer[:, 1:2], in_=table_warmer[:, 0:1], func=ACT.Silu)
        decay = {}

        def make_decay(w):
            table = const.tile([P, width], F32, name="decay_" + str(w))
            decay[w] = table
            if w == 1:
                nc.vector.tensor_tensor(out=table[:], in0=falling[:], in1=rising[:], op=MIN)
            else:
                near = rising if w == 0 else falling
                nc.gpsimd.tensor_scalar(
                    out=table[:], in0=near[:], scalar1=GAMMA**BANK, scalar2=0.0, op0=MULT, op1=ADD
                )

        operand = {}
        in_progress = {}
        quantised = set()
        completed = []

        def prepare(n, on_vector):
            b, step = divmod(n, STEPS)
            if step < TRANSPOSE_STEPS:
                name, half = sources(b)[step // 2]
                part, parts = step % 2, 2
            else:
                name, half = "v", (step - TRANSPOSE_STEPS) // (H // P)
                part, parts = (step - TRANSPOSE_STEPS) % (H // P), H // P
            if half == 0 and part == 0:
                codes = operands.tile([P, S], U32, align_bytes=64, name=name + "_codes")
                scales = operands.tile([P, S], U8, align_bytes=64, name=name + "_scales")
                operand[(name, b)] = (codes, scales)
            if part == 0:
                grouped = stage.tile([P, BANK * PACK], BF16, align_bytes=64, bufs=4)
                in_progress["grouped"] = grouped
            grouped = in_progress["grouped"]

            bank = psum.tile([P, 4, P], F32, tag="bank")
            if name == "v":
                assert ("x", b, half) in quantised
                x_codes, x_scales = operand[("x", b)]
                cols = slice(part * P, (part + 1) * P)
                for t in range(PACK):
                    tokens = slice((half * TILES + t) * P, (half * TILES + t + 1) * P)
                    nc.tensor.matmul_mx(
                        out=bank[:, t, :],
                        lhsT=x_codes[:, tokens].bitcast(FP8X4),
                        lhsT_scale=x_scales[:, tokens],
                        rhs=w_codes[:, cols].bitcast(FP8X4),
                        rhs_scale=w_scales[:, cols],
                        start=True,
                        stop=True,
                    )
                source = bank[:].rearrange("p t h -> p h t")
                target = grouped[:].rearrange("p (h t) -> p h t", t=PACK)[:, cols, :]
            else:
                if 0 < n < WARM_STEPS:
                    nc.tensor.matmul(bank[:, 0:3, :], lhsT=zeros[:, :P], rhs=zeros[:, : 3 * P], start=True, stop=True)
                words = rows[(name, b)][:, half].bitcast(F32)
                for j in range(2):
                    for u in range(2):
                        word_cols = slice(u, H // 2, 2) if name == "x" else slice(u * P, (u + 1) * P)
                        nc.tensor.transpose(bank[:, 2 * j + u, :], words[:, 2 * part + j, word_cols], identity[:])
                source = bank[:].rearrange("p (j u) r -> p j r u", u=2)
                target = grouped[:].bitcast(F32).rearrange("p (j r u) -> p j r u", r=P, u=2)
                target = target[:, 2 * part : 2 * part + 2]
            if on_vector:
                nc.vector.tensor_copy(out=target, in_=source)
            else:
                nc.scalar.copy(out=target, in_=source)
            if part == parts - 1:
                completed.append((name, b, half, grouped))

        def quantise_next():
            name, b, half, grouped = completed[0]
            completed.remove(completed[0])
            codes, scales = operand[(name, b)]
            cols = slice(half * BANK, (half + 1) * BANK)
            nc.vector.quantize_mx(out=codes[:, cols].bitcast(FP8X4), scales=scales[:, cols], in_=grouped[:])
            quantised.add((name, b, half))

        def unit_of(u):
            b, rest = divmod(u, HALVES * HALVES)
            query_half, key_half = divmod(rest, HALVES)
            return b, query_half, key_half

        score_banks = {}

        def score_pass(k):
            u, t = divmod(k, PACK)
            b, query_half, key_half = unit_of(u)
            assert ("k", b, key_half) in quantised and ("q", b, query_half) in quantised
            k_codes, k_scales = operand[("k", b)]
            q_codes, q_scales = operand[("q", b)]
            queries = slice(query_half * BANK, (query_half + 1) * BANK)
            keys = slice((key_half * TILES + t) * P, (key_half * TILES + t + 1) * P)
            scores = psum.tile([P, BANK], F32, tag="bank")
            nc.tensor.matmul_mx(
                out=scores[:],
                lhsT=k_codes[:, keys].bitcast(FP8X4),
                lhsT_scale=k_scales[:, keys],
                rhs=q_codes[:, queries].bitcast(FP8X4),
                rhs_scale=q_scales[:, queries],
                start=True,
                stop=True,
            )
            score_banks[k] = scores

        decayed_of = {}

        def apply_decay(k):
            u, t = divmod(k, PACK)
            b, query_half, key_half = unit_of(u)
            w = query_half - key_half + HALVES - 1
            if t == 0:
                decayed = stage.tile([P, PACK, BANK], F32)
                decayed_of[u] = decayed
            first = PACK - 1 - t
            nc.vector.tensor_tensor(
                out=decayed_of[u][:, t, :],
                in0=score_banks[k][:],
                in1=decay[w][:, first : first + BANK],
                op=MULT,
            )

        gated_of = {}

        def swish(u, piece, pieces):
            if piece == 0:
                gated = stage.tile([P, BANK, PACK], BF16, align_bytes=64)
                gated_of[u] = gated
            queries = slice(piece * BANK // pieces, (piece + 1) * BANK // pieces)
            nc.scalar.activation(
                out=gated_of[u][:, queries, :].rearrange("p (s i) t -> p s t i", i=2),
                in_=decayed_of[u][:, :, queries].rearrange("p t (s i) -> p s t i", i=2),
                func=ACT.Silu,
            )

        gates = {}

        def quantise_gates(u, piece, pieces):
            b, query_half, key_half = unit_of(u)
            if key_half == 0 and piece == 0:
                g_codes = operands.tile([P, HALVES, BANK], U32, align_bytes=64, bufs=3)
                g_scales = operands.tile([P, HALVES, BANK], U8, align_bytes=64, bufs=3)
                gates[(b, query_half)] = (g_codes, g_scales)
            g_codes, g_scales = gates[(b, query_half)]
            queries = slice(piece * BANK // pieces, (piece + 1) * BANK // pieces)
            nc.vector.quantize_mx(
                out=g_codes[:, key_half, queries].bitcast(FP8X4),
                scales=g_scales[:, key_half, queries],
                in_=gated_of[u][:, queries, :].rearrange("p m t -> p (m t)"),
            )

        out_banks = {}

        def out_pass(o, key_half):
            b, tile_in_sequence = divmod(o, S // P)
            query_half, j = divmod(tile_in_sequence, TILES)
            assert ("v", b, key_half) in quantised
            g_codes, g_scales = gates[(b, query_half)]
            v_codes, v_scales = operand[("v", b)]
            queries = slice(j * P, (j + 1) * P)
            tokens = slice(key_half * BANK, (key_half + 1) * BANK)
            if key_half == 0:
                acc = psum.tile([P, H], F32, tag="bank")
                out_banks[o] = acc
            nc.tensor.matmul_mx(
                out=out_banks[o][:],
                lhsT=g_codes[:, key_half, queries].bitcast(FP8X4),
                lhsT_scale=g_scales[:, key_half, queries],
                rhs=v_codes[:, tokens].bitcast(FP8X4),
                rhs_scale=v_scales[:, tokens],
                start=(key_half == 0),
                stop=(key_half == HALVES - 1),
            )

        def store_out(o, on_vector):
            b, tile_in_sequence = divmod(o, S // P)
            result = stage.tile([P, H], F32, bufs=OUT_TILES)
            if on_vector:
                nc.vector.tensor_copy(out=result[:], in_=out_banks[o][:])
            else:
                nc.scalar.copy(out=result[:], in_=out_banks[o][:])
            nc.sync.dma_start(out=out[b, tile_in_sequence * P : (tile_in_sequence + 1) * P, :], in_=result[:])

        def out_tile(o, on_vector):
            for key_half in range(HALVES):
                out_pass(o, key_half)
            store_out(o, on_vector)

        def steps_due(r):
            return min(12 + 6 * r if r < 3 else 15 + 5 * r, B * STEPS)

        def outs_due(r):
            if r >= UNITS - 1:
                return OUT_TILES - TILES - 2
            return max(0, 2 * (r - 2))

        def on_vector(n):
            return n % 5 == 0

        def out_on_vector(o):
            return o % 3 == 2

        for n in range(3):
            prepare(n, True)
        quantise_next()
        prepare(3, False)
        quantise_next()
        for n in range(4, 6):
            prepare(n, False)
        make_decay(1)
        make_decay(0)
        make_decay(2)
        prepare(6, False)
        for t in range(PACK):
            if t == 2:
                prepare(7, False)
            score_pass(t)
        done = 8
        outs = 0
        for r in range(UNITS):
            if r > 0:
                swish(r - 1, 0, 1)
            for t in range(PACK):
                apply_decay(PACK * r + t)
                if t % 2 == 1 and completed:
                    quantise_next()
            while r > 0 and completed:
                quantise_next()
            while done < steps_due(r) or outs < outs_due(r):
                for i in range(2):
                    if done < steps_due(r):
                        prepare(done, on_vector(done))
                        done += 1
                while outs < outs_due(r):
                    out_tile(outs, out_on_vector(outs))
                    outs += 1
            if r > 0:
                quantise_gates(r - 1, 0, 1)
            else:
                quantise_next()
            if r + 1 < UNITS:
                for t in range(PACK):
                    score_pass(PACK * (r + 1) + t)
        last = OUT_TILES - TILES
        for piece in range(TILES):
            swish(UNITS - 1, piece, TILES)
        for o in range(outs, last):
            out_tile(o, True)
        for piece in range(TILES):
            out_pass(last + piece, 0)
        for piece in range(TILES):
            quantise_gates(UNITS - 1, piece, TILES)
            out_pass(last + piece, 1)
            if piece == 1:
                store_out(last, True)
        store_out(last + 1, False)
        store_out(last + 2, True)
        store_out(last + 3, False)
